import numpy as np
import ml_dtypes


def mxq(x, axis, fmt="e4m3"):
    dtype, down = {"e4m3": (ml_dtypes.float8_e4m3fn, 7), "e5m2": (ml_dtypes.float8_e5m2, 14)}[fmt]
    v = np.moveaxis(np.asarray(x, np.float32).astype(ml_dtypes.bfloat16).astype(np.float64), axis, -1)
    blocks = v.reshape(v.shape[:-1] + (-1, 32))
    amax = np.abs(blocks).max(-1, keepdims=True)
    byte = np.maximum(np.where(amax > 0, np.frexp(amax)[1] - 1 + 127, 0) - down, 1)
    scale = np.exp2(byte - 127.0)
    codes = (blocks / scale).astype(np.float32).astype(dtype).astype(np.float64)
    return np.moveaxis((codes * scale).reshape(v.shape), -1, axis)


WIDE = False


def mx_kscale(k):
    if not WIDE:
        return np.ones(k)
    levels = np.array([10, -10, 5, -5, 0])
    a = np.random.permutation(np.resize(levels, k // 512 * 4)).reshape(k // 512, 4)
    idx = np.arange(k)
    return np.exp2(a[idx // 512, idx % 128 // 32])


BF16 = ml_dtypes.bfloat16


def bf(x):
    return np.asarray(x, np.float32).astype(BF16)


def f64(x):
    return np.asarray(x).astype(np.float64)


B, C, H, W, P = 4, 1024, 64, 32, 1024
HP, WP = H // 2, W // 2
M = HP * WP
EPS = 1e-5


def maxpool2x2(x):
    return x.reshape(B, C, HP, 2, WP, 2).max(axis=(3, 5))


def setup_inputs():
    s = mx_kscale(C)
    return {'x': bf(np.random.standard_normal((B, C, H, W)) * s[None, :, None, None]),
            'wk': bf(np.random.standard_normal((P, C)) / np.sqrt(C) / s[None, :]),
            'bk': bf(np.random.standard_normal(P) * 0.1),
            'wv': bf(np.random.standard_normal((P, C)) / np.sqrt(C) / s[None, :]),
            'bv': bf(np.random.standard_normal(P) * 0.1),
            'k_gamma': bf(np.random.uniform(0.5, 1.5, P)),
            'k_beta': bf(np.random.standard_normal(P) * 0.1),
            'k_mean': bf(np.random.standard_normal(P) * 0.1),
            'k_var': bf(np.random.uniform(0.5, 1.5, P))}


def reference(x, wk, bk, wv, bv, k_gamma, k_beta, k_mean, k_var):
    xp = mxq(maxpool2x2(f64(x)).reshape(B, C, M), 1, 'e4m3')
    k = (mxq(f64(wk), 1, 'e4m3') @ xp) + f64(bk)[None, :, None]
    sc = f64(k_gamma) / np.sqrt(f64(k_var) + EPS)
    k = (k - f64(k_mean)[None, :, None]) * sc[None, :, None] + f64(k_beta)[None, :, None]
    v = (mxq(f64(wv), 1, 'e4m3') @ xp) + f64(bv)[None, :, None]
    return k.reshape(B, P, HP, WP), v.reshape(B, P, HP, WP)

@@ -1,0 +1,163 @@
+from contextlib import ExitStack
+
+import concourse.mybir as mybir
+from concourse.masks import make_identity
+
+BF16 = mybir.dt.bfloat16
+F32 = mybir.dt.float32
+U32 = mybir.dt.uint32
+U8 = mybir.dt.uint8
+FP8X4 = mybir.dt.float8_e4m3fn_x4
+ACT = mybir.ActivationFunctionType
+
+P = 128
+PACK = 4
+K_PASS = P * PACK
+
+B, C, H, W = 4, 1024, 64, 32
+O = 1024
+M = (H // 2) * (W // 2)
+PASSES = C // K_PASS
+O_TILES = O // P
+EPS = 1e-5
+
+FLOPS = 2 * 2 * B * O * C * M
+
+RAW_COLS = PACK * H * W
+assert RAW_COLS == O_TILES * C
+
+BK, BV, GAMMA, BETA, MEAN, VAR = 0, 1, 2, 3, 4, 5
+
+
+def tile_nonlocalnd_bn_pa_t_kernel(
+    tc, x, wk, bk, wv, bv, k_gamma, k_beta, k_mean, k_var, out_0, out_1
+):
+    nc = tc.nc
+    with ExitStack() as ctx:
+        const = ctx.enter_context(tc.tile_pool(name="const", bufs=1))
+        loads = ctx.enter_context(tc.tile_pool(name="loads", bufs=6))
+        work = ctx.enter_context(tc.tile_pool(name="work", bufs=2))
+        keep = ctx.enter_context(tc.tile_pool(name="keep", bufs=1))
+        results = ctx.enter_context(tc.tile_pool(name="results", bufs=3))
+        psum = ctx.enter_context(tc.psum_pool(name="psum", bufs=8))
+
+        def load(src):
+            raw = loads.tile([P, RAW_COLS], BF16, tag="raw")
+            nc.sync.dma_start(out=raw[:], in_=src)
+            return raw
+
+        def load_image(b):
+            tiles = x[b].rearrange("(g p j) h w -> g p (j h w)", p=P, j=PACK)
+            return [load(tiles[g]) for g in range(PASSES)]
+
+        def load_weight(w):
+            return load(w.rearrange("(p t) c -> p (t c)", t=O_TILES))
+
+        def pool_and_quantise(x_raw):
+            xp_codes = work.tile([P, PASSES, M], U32, align_bytes=64)
+            xp_scales = work.tile([P, PASSES, M], U8, align_bytes=64)
+            for g in range(PASSES):
+                rows = x_raw[g][:].rearrange("p (r d w) -> p r d w", d=2, w=W)
+                row_max = work.tile([P, RAW_COLS // 2], BF16)
+                nc.vector.tensor_max(
+                    out=row_max[:].rearrange("p (r w) -> p r w", w=W),
+                    in0=rows[:, :, 0, :],
+                    in1=rows[:, :, 1, :],
+                )
+                pairs = row_max[:].rearrange("p (j m d) -> p m j d", j=PACK, d=2)
+                grouped = work.tile([P, M, PACK], BF16, align_bytes=64)
+                nc.vector.tensor_max(out=grouped[:], in0=pairs[:, :, :, 0], in1=pairs[:, :, :, 1])
+                nc.vector.quantize_mx(
+                    out=xp_codes[:, g, :].bitcast(FP8X4),
+                    scales=xp_scales[:, g, :],
+                    in_=grouped[:].rearrange("p m j -> p (m j)"),
+                )
+            return xp_codes, xp_scales
+
+        def quantise_weight(w_raw, name):
+            w_codes = keep.tile([P, PASSES, O], U32, name=name + "_codes", align_bytes=64)
+            w_scales = keep.tile([P, PASSES, O], U8, name=name + "_scales", align_bytes=64)
+            words = w_raw[:].bitcast(F32).rearrange(
+                "i (t g q u) -> i t g u q", t=O_TILES, g=PASSES, u=2
+            )
+            for g in range(PASSES):
+                w_grouped = work.tile([P, O_TILES, P, PACK], BF16, align_bytes=64)
+                grouped_words = w_grouped[:].bitcast(F32)
+                for t in range(0, O_TILES, 2):
+                    bank = psum.tile([P, 2, 2, P], F32, tag="bank")
+                    for d in range(2):
+                        for u in range(2):
+                            nc.tensor.transpose(bank[:, d, u, :], words[:, t + d, g, u, :], ident[:])
+                    nc.scalar.copy(
+                        out=grouped_words[:, t : t + 2, :, :],
+                        in_=bank[:].rearrange("q d u i -> q d i u"),
+                    )
+                nc.vector.quantize_mx(
+                    out=w_codes[:, g, :].bitcast(FP8X4),
+                    scales=w_scales[:, g, :],
+                    in_=w_grouped[:].rearrange("q t i j -> q (t i j)"),
+                )
+            return w_codes, w_scales
+
+        def convolve(b, xp, weight, scale, shift, out):
+            xp_codes, xp_scales = xp
+            w_codes, w_scales = weight
+            result = results.tile([P, O_TILES, M], F32)
+            for t in range(O_TILES):
+                cols = slice(t * P, (t + 1) * P)
+                acc = psum.tile([P, M], F32, tag="bank")
+                for g in range(PASSES):
+                    nc.tensor.matmul_mx(
+                        out=acc[:],
+                        lhsT=w_codes[:, g, cols].bitcast(FP8X4),
+                        lhsT_scale=w_scales[:, g, cols],
+                        rhs=xp_codes[:, g, :].bitcast(FP8X4),
+                        rhs_scale=xp_scales[:, g, :],
+                        start=(g == 0),
+                        stop=(g == PASSES - 1),
+                    )
+                nc.scalar.activation(
+                    out=result[:, t, :],
+                    in_=acc[:],
+                    func=ACT.Identity,
+                    scale=scale if isinstance(scale, float) else scale[:, t : t + 1],
+                    bias=shift[:, t : t + 1],
+                )
+            nc.scalar.dma_start(
+                out=out[b].rearrange("(p t) h w -> p (t h w)", t=O_TILES),
+                in_=result[:].rearrange("p t m -> p (t m)"),
+            )
+
+        x_raw = load_image(0)
+        wk_raw = load_weight(wk)
+        wv_raw = load_weight(wv)
+
+        ident = const.tile([P, P], F32)
+        make_identity(nc, ident[:])
+        par_raw = const.tile([P, 6, 16], BF16)
+        for row, vec in ((BK, bk), (BV, bv), (GAMMA, k_gamma), (BETA, k_beta), (MEAN, k_mean), (VAR, k_var)):
+            nc.gpsimd.dma_start(
+                out=par_raw[:, row, 0:O_TILES], in_=vec.rearrange("(p t) -> p t", t=O_TILES)
+            )
+        par = const.tile([P, 6, O_TILES], F32)
+        nc.vector.tensor_copy(out=par[:], in_=par_raw[:, :, 0:O_TILES])
+        k_scale = const.tile([P, O_TILES], F32)
+        k_shift = const.tile([P, O_TILES], F32)
+        nc.vector.tensor_scalar_add(out=k_scale[:], in0=par[:, VAR, :], scalar1=EPS)
+        nc.scalar.sqrt(k_scale[:], k_scale[:])
+        nc.vector.reciprocal(out=k_scale[:], in_=k_scale[:])
+        nc.vector.tensor_mul(out=k_scale[:], in0=k_scale[:], in1=par[:, GAMMA, :])
+        nc.vector.tensor_sub(out=k_shift[:], in0=par[:, BK, :], in1=par[:, MEAN, :])
+        nc.vector.tensor_mul(out=k_shift[:], in0=k_shift[:], in1=k_scale[:])
+        nc.vector.tensor_add(out=k_shift[:], in0=k_shift[:], in1=par[:, BETA, :])
+
+        xp = pool_and_quantise(x_raw)
+        k_weight = quantise_weight(wk_raw, "wk")
+        v_weight = quantise_weight(wv_raw, "wv")
+        for b in range(B):
+            if b + 1 < B:
+                x_raw = load_image(b + 1)
+            convolve(b, xp, k_weight, k_scale, k_shift, out_0)
+            convolve(b, xp, v_weight, 1.0, par[:, BV, :], out_1)
+            if b + 1 < B:
+                xp = pool_and_quantise(x_raw)

@@ -35,7 +35,7 @@ def tile_nonlocalnd_bn_pa_t_kernel(
     nc = tc.nc
     with ExitStack() as ctx:
         const = ctx.enter_context(tc.tile_pool(name="const", bufs=1))
-        loads = ctx.enter_context(tc.tile_pool(name="loads", bufs=6))
+        loads = ctx.enter_context(tc.tile_pool(name="loads", bufs=8))
         work = ctx.enter_context(tc.tile_pool(name="work", bufs=2))
         keep = ctx.enter_context(tc.tile_pool(name="keep", bufs=1))
         results = ctx.enter_context(tc.tile_pool(name="results", bufs=3))
@@ -80,29 +80,29 @@ def tile_nonlocalnd_bn_pa_t_kernel(
             words = w_raw[:].bitcast(F32).rearrange(
                 "i (t g q u) -> i t g u q", t=O_TILES, g=PASSES, u=2
             )
+            w_grouped = results.tile([P, PASSES, O_TILES, P, PACK], BF16, tag="result", align_bytes=64)
+            grouped_words = w_grouped[:].bitcast(F32)
             for g in range(PASSES):
-                w_grouped = work.tile([P, O_TILES, P, PACK], BF16, align_bytes=64)
-                grouped_words = w_grouped[:].bitcast(F32)
                 for t in range(0, O_TILES, 2):
                     bank = psum.tile([P, 2, 2, P], F32, tag="bank")
                     for d in range(2):
                         for u in range(2):
                             nc.tensor.transpose(bank[:, d, u, :], words[:, t + d, g, u, :], ident[:])
                     nc.scalar.copy(
-                        out=grouped_words[:, t : t + 2, :, :],
+                        out=grouped_words[:, g, t : t + 2, :, :],
                         in_=bank[:].rearrange("q d u i -> q d i u"),
                     )
                 nc.vector.quantize_mx(
                     out=w_codes[:, g, :].bitcast(FP8X4),
                     scales=w_scales[:, g, :],
-                    in_=w_grouped[:].rearrange("q t i j -> q (t i j)"),
+                    in_=w_grouped[:, g, :, :, :].rearrange("q t i j -> q (t i j)"),
                 )
             return w_codes, w_scales
 
         def convolve(b, xp, weight, scale, shift, out):
             xp_codes, xp_scales = xp
             w_codes, w_scales = weight
-            result = results.tile([P, O_TILES, M], F32)
+            result = results.tile([P, O_TILES, M], F32, tag="result", align_bytes=64)
             for t in range(O_TILES):
                 cols = slice(t * P, (t + 1) * P)
                 acc = psum.tile([P, M], F32, tag="bank")
@@ -123,41 +123,46 @@ def tile_nonlocalnd_bn_pa_t_kernel(
                     scale=scale if isinstance(scale, float) else scale[:, t : t + 1],
                     bias=shift[:, t : t + 1],
                 )
-            nc.scalar.dma_start(
+            nc.sync.dma_start(
                 out=out[b].rearrange("(p t) h w -> p (t h w)", t=O_TILES),
                 in_=result[:].rearrange("p t m -> p (t m)"),
             )
 
-        x_raw = load_image(0)
+        def fold_batch_norm():
+            par = const.tile([P, 6, O_TILES], F32)
+            nc.vector.tensor_copy(out=par[:], in_=par_raw[:, :, 0:O_TILES])
+            k_scale = const.tile([P, O_TILES], F32)
+            k_shift = const.tile([P, O_TILES], F32)
+            nc.vector.tensor_scalar_add(out=k_scale[:], in0=par[:, VAR, :], scalar1=EPS)
+            nc.scalar.sqrt(k_scale[:], k_scale[:])
+            nc.vector.reciprocal(out=k_scale[:], in_=k_scale[:])
+            nc.vector.tensor_mul(out=k_scale[:], in0=k_scale[:], in1=par[:, GAMMA, :])
+            nc.vector.tensor_sub(out=k_shift[:], in0=par[:, BK, :], in1=par[:, MEAN, :])
+            nc.vector.tensor_mul(out=k_shift[:], in0=k_shift[:], in1=k_scale[:])
+            nc.vector.tensor_add(out=k_shift[:], in0=k_shift[:], in1=par[:, BETA, :])
+            return k_scale, k_shift, par[:, BV, :]
+
+        x_raw = [load_image(0)]
         wk_raw = load_weight(wk)
         wv_raw = load_weight(wv)
+        x_raw.append(load_image(1))
+        x_raw.append(load_image(2))
 
         ident = const.tile([P, P], F32)
         make_identity(nc, ident[:])
         par_raw = const.tile([P, 6, 16], BF16)
         for row, vec in ((BK, bk), (BV, bv), (GAMMA, k_gamma), (BETA, k_beta), (MEAN, k_mean), (VAR, k_var)):
-            nc.gpsimd.dma_start(
+            nc.scalar.dma_start(
                 out=par_raw[:, row, 0:O_TILES], in_=vec.rearrange("(p t) -> p t", t=O_TILES)
             )
-        par = const.tile([P, 6, O_TILES], F32)
-        nc.vector.tensor_copy(out=par[:], in_=par_raw[:, :, 0:O_TILES])
-        k_scale = const.tile([P, O_TILES], F32)
-        k_shift = const.tile([P, O_TILES], F32)
-        nc.vector.tensor_scalar_add(out=k_scale[:], in0=par[:, VAR, :], scalar1=EPS)
-        nc.scalar.sqrt(k_scale[:], k_scale[:])
-        nc.vector.reciprocal(out=k_scale[:], in_=k_scale[:])
-        nc.vector.tensor_mul(out=k_scale[:], in0=k_scale[:], in1=par[:, GAMMA, :])
-        nc.vector.tensor_sub(out=k_shift[:], in0=par[:, BK, :], in1=par[:, MEAN, :])
-        nc.vector.tensor_mul(out=k_shift[:], in0=k_shift[:], in1=k_scale[:])
-        nc.vector.tensor_add(out=k_shift[:], in0=k_shift[:], in1=par[:, BETA, :])
 
-        xp = pool_and_quantise(x_raw)
+        xp = pool_and_quantise(x_raw[0])
+        x_raw.append(load_image(3))
+        k_scale, k_shift, v_shift = fold_batch_norm()
         k_weight = quantise_weight(wk_raw, "wk")
         v_weight = quantise_weight(wv_raw, "wv")
         for b in range(B):
-            if b + 1 < B:
-                x_raw = load_image(b + 1)
             convolve(b, xp, k_weight, k_scale, k_shift, out_0)
-            convolve(b, xp, v_weight, 1.0, par[:, BV, :], out_1)
+            convolve(b, xp, v_weight, 1.0, v_shift, out_1)
             if b + 1 < B:
-                xp = pool_and_quantise(x_raw)
+                xp = pool_and_quantise(x_raw[b + 1])

@@ -35,10 +35,10 @@ def tile_nonlocalnd_bn_pa_t_kernel(
     nc = tc.nc
     with ExitStack() as ctx:
         const = ctx.enter_context(tc.tile_pool(name="const", bufs=1))
-        loads = ctx.enter_context(tc.tile_pool(name="loads", bufs=8))
+        loads = ctx.enter_context(tc.tile_pool(name="loads", bufs=6))
         work = ctx.enter_context(tc.tile_pool(name="work", bufs=2))
         keep = ctx.enter_context(tc.tile_pool(name="keep", bufs=1))
-        results = ctx.enter_context(tc.tile_pool(name="results", bufs=3))
+        results = ctx.enter_context(tc.tile_pool(name="results", bufs=5))
         psum = ctx.enter_context(tc.psum_pool(name="psum", bufs=8))
 
         def load(src):
@@ -146,7 +146,6 @@ def tile_nonlocalnd_bn_pa_t_kernel(
         wk_raw = load_weight(wk)
         wv_raw = load_weight(wv)
         x_raw.append(load_image(1))
-        x_raw.append(load_image(2))
 
         ident = const.tile([P, P], F32)
         make_identity(nc, ident[:])
@@ -157,10 +156,11 @@ def tile_nonlocalnd_bn_pa_t_kernel(
             )
 
         xp = pool_and_quantise(x_raw[0])
-        x_raw.append(load_image(3))
+        x_raw.append(load_image(2))
         k_scale, k_shift, v_shift = fold_batch_norm()
         k_weight = quantise_weight(wk_raw, "wk")
         v_weight = quantise_weight(wv_raw, "wv")
+        x_raw.append(load_image(3))
         for b in range(B):
             convolve(b, xp, k_weight, k_scale, k_shift, out_0)
             convolve(b, xp, v_weight, 1.0, v_shift, out_1)

@@ -130,7 +130,7 @@ def tile_nonlocalnd_bn_pa_t_kernel(
 
         def fold_batch_norm():
             par = const.tile([P, 6, O_TILES], F32)
-            nc.vector.tensor_copy(out=par[:], in_=par_raw[:, :, 0:O_TILES])
+            nc.vector.tensor_copy(out=par[:], in_=par_raw[:, :, 0:6].rearrange("p t r -> p r t"))
             k_scale = const.tile([P, O_TILES], F32)
             k_shift = const.tile([P, O_TILES], F32)
             nc.vector.tensor_scalar_add(out=k_scale[:], in0=par[:, VAR, :], scalar1=EPS)
@@ -149,11 +149,16 @@ def tile_nonlocalnd_bn_pa_t_kernel(
 
         ident = const.tile([P, P], F32)
         make_identity(nc, ident[:])
-        par_raw = const.tile([P, 6, 16], BF16)
+        par_rows = const.tile([P, O], BF16)
+        nc.vector.memset(par_rows[:], 0.0)
         for row, vec in ((BK, bk), (BV, bv), (GAMMA, k_gamma), (BETA, k_beta), (MEAN, k_mean), (VAR, k_var)):
-            nc.scalar.dma_start(
-                out=par_raw[:, row, 0:O_TILES], in_=vec.rearrange("(p t) -> p t", t=O_TILES)
-            )
+            nc.scalar.dma_start(out=par_rows[row : row + 1, :], in_=vec.rearrange("(a o) -> a o", a=1))
+        ident_bf = const.tile([P, P], BF16)
+        make_identity(nc, ident_bf[:])
+        par_raw = psum.tile([P, O_TILES, P], BF16, tag="bank")
+        par_cols = par_rows[:].rearrange("r (p t) -> r t p", t=O_TILES)
+        for t in range(O_TILES):
+            nc.tensor.transpose(par_raw[:, t, :], par_cols[:, t, :], ident_bf[:])
 
         xp = pool_and_quantise(x_raw[0])
         x_raw.append(load_image(2))

@@ -25,6 +25,7 @@ FLOPS = 2 * 2 * B * O * C * M
 
 RAW_COLS = PACK * H * W
 assert RAW_COLS == O_TILES * C
+SLOTS = 11
 
 BK, BV, GAMMA, BETA, MEAN, VAR = 0, 1, 2, 3, 4, 5
 
@@ -35,14 +36,19 @@ def tile_nonlocalnd_bn_pa_t_kernel(
     nc = tc.nc
     with ExitStack() as ctx:
         const = ctx.enter_context(tc.tile_pool(name="const", bufs=1))
-        loads = ctx.enter_context(tc.tile_pool(name="loads", bufs=6))
+        slots = ctx.enter_context(tc.tile_pool(name="slots", bufs=1))
+        taken = []
+
+        def next_slot():
+            taken.append(None)
+            return "slot%d" % ((len(taken) - 1) % SLOTS)
+
         work = ctx.enter_context(tc.tile_pool(name="work", bufs=2))
         keep = ctx.enter_context(tc.tile_pool(name="keep", bufs=1))
-        results = ctx.enter_context(tc.tile_pool(name="results", bufs=5))
         psum = ctx.enter_context(tc.psum_pool(name="psum", bufs=8))
 
         def load(src):
-            raw = loads.tile([P, RAW_COLS], BF16, tag="raw")
+            raw = slots.tile([P, RAW_COLS], BF16, tag=next_slot(), align_bytes=64)
             nc.sync.dma_start(out=raw[:], in_=src)
             return raw
 
@@ -80,7 +86,7 @@ def tile_nonlocalnd_bn_pa_t_kernel(
             words = w_raw[:].bitcast(F32).rearrange(
                 "i (t g q u) -> i t g u q", t=O_TILES, g=PASSES, u=2
             )
-            w_grouped = results.tile([P, PASSES, O_TILES, P, PACK], BF16, tag="result", align_bytes=64)
+            w_grouped = slots.tile([P, PASSES, O_TILES, P, PACK], BF16, tag=next_slot(), align_bytes=64)
             grouped_words = w_grouped[:].bitcast(F32)
             for g in range(PASSES):
                 for t in range(0, O_TILES, 2):
@@ -102,7 +108,7 @@ def tile_nonlocalnd_bn_pa_t_kernel(
         def convolve(b, xp, weight, scale, shift, out):
             xp_codes, xp_scales = xp
             w_codes, w_scales = weight
-            result = results.tile([P, O_TILES, M], F32, tag="result", align_bytes=64)
+            result = slots.tile([P, O_TILES, M], F32, tag=next_slot(), align_bytes=64)
             for t in range(O_TILES):
                 cols = slice(t * P, (t + 1) * P)
                 acc = psum.tile([P, M], F32, tag="bank")
@@ -146,6 +152,7 @@ def tile_nonlocalnd_bn_pa_t_kernel(
         wk_raw = load_weight(wk)
         wv_raw = load_weight(wv)
         x_raw.append(load_image(1))
+        x_raw.append(load_image(2))
 
         ident = const.tile([P, P], F32)
         make_identity(nc, ident[:])
@@ -161,7 +168,6 @@ def tile_nonlocalnd_bn_pa_t_kernel(
             nc.tensor.transpose(par_raw[:, t, :], par_cols[:, t, :], ident_bf[:])
 
         xp = pool_and_quantise(x_raw[0])
-        x_raw.append(load_image(2))
         k_scale, k_shift, v_shift = fold_batch_norm()
         k_weight = quantise_weight(wk_raw, "wk")
         v_weight = quantise_weight(wv_raw, "wv")

@@ -48,7 +48,7 @@ def tile_nonlocalnd_bn_pa_t_kernel(
         psum = ctx.enter_context(tc.psum_pool(name="psum", bufs=8))
 
         def load(src):
-            raw = slots.tile([P, RAW_COLS], BF16, tag=next_slot(), align_bytes=64)
+            raw = slots.tile([P, RAW_COLS], BF16, tag=next_slot(), align_bytes=256)
             nc.sync.dma_start(out=raw[:], in_=src)
             return raw
 
@@ -86,7 +86,7 @@ def tile_nonlocalnd_bn_pa_t_kernel(
             words = w_raw[:].bitcast(F32).rearrange(
                 "i (t g q u) -> i t g u q", t=O_TILES, g=PASSES, u=2
             )
-            w_grouped = slots.tile([P, PASSES, O_TILES, P, PACK], BF16, tag=next_slot(), align_bytes=64)
+            w_grouped = slots.tile([P, PASSES, O_TILES, P, PACK], BF16, tag=next_slot(), align_bytes=256)
             grouped_words = w_grouped[:].bitcast(F32)
             for g in range(PASSES):
                 for t in range(0, O_TILES, 2):
@@ -108,7 +108,7 @@ def tile_nonlocalnd_bn_pa_t_kernel(
         def convolve(b, xp, weight, scale, shift, out):
             xp_codes, xp_scales = xp
             w_codes, w_scales = weight
-            result = slots.tile([P, O_TILES, M], F32, tag=next_slot(), align_bytes=64)
+            result = slots.tile([P, O_TILES, M], F32, tag=next_slot(), align_bytes=256)
             for t in range(O_TILES):
                 cols = slice(t * P, (t + 1) * P)
                 acc = psum.tile([P, M], F32, tag="bank")

@@ -149,6 +149,10 @@ def tile_nonlocalnd_bn_pa_t_kernel(
             return k_scale, k_shift, par[:, BV, :]
 
         x_raw = [load_image(0)]
+        par_rows = const.tile([P, O], BF16)
+        nc.vector.memset(par_rows[:], 0.0)
+        for row, vec in ((BK, bk), (BV, bv), (GAMMA, k_gamma), (BETA, k_beta), (MEAN, k_mean), (VAR, k_var)):
+            nc.sync.dma_start(out=par_rows[row : row + 1, :], in_=vec.rearrange("(a o) -> a o", a=1))
         wk_raw = load_weight(wk)
         wv_raw = load_weight(wv)
         x_raw.append(load_image(1))
@@ -156,10 +160,6 @@ def tile_nonlocalnd_bn_pa_t_kernel(
 
         ident = const.tile([P, P], F32)
         make_identity(nc, ident[:])
-        par_rows = const.tile([P, O], BF16)
-        nc.vector.memset(par_rows[:], 0.0)
-        for row, vec in ((BK, bk), (BV, bv), (GAMMA, k_gamma), (BETA, k_beta), (MEAN, k_mean), (VAR, k_var)):
-            nc.scalar.dma_start(out=par_rows[row : row + 1, :], in_=vec.rearrange("(a o) -> a o", a=1))
         ident_bf = const.tile([P, P], BF16)
         make_identity(nc, ident_bf[:])
         par_raw = psum.tile([P, O_TILES, P], BF16, tag="bank")

@@ -129,7 +129,8 @@ def tile_nonlocalnd_bn_pa_t_kernel(
                     scale=scale if isinstance(scale, float) else scale[:, t : t + 1],
                     bias=shift[:, t : t + 1],
                 )
-            nc.sync.dma_start(
+            queue = nc.scalar if (out is out_1 and b >= 1) else nc.sync
+            queue.dma_start(
                 out=out[b].rearrange("(p t) h w -> p (t h w)", t=O_TILES),
                 in_=result[:].rearrange("p t m -> p (t m)"),
             )

from contextlib import ExitStack

import concourse.mybir as mybir
from concourse.masks import make_identity

BF16 = mybir.dt.bfloat16
F32 = mybir.dt.float32
U32 = mybir.dt.uint32
U8 = mybir.dt.uint8
FP8X4 = mybir.dt.float8_e4m3fn_x4
ACT = mybir.ActivationFunctionType

P = 128
PACK = 4
K_PASS = P * PACK

B, C, H, W = 4, 1024, 64, 32
O = 1024
M = (H // 2) * (W // 2)
PASSES = C // K_PASS
O_TILES = O // P
EPS = 1e-5

FLOPS = 2 * 2 * B * O * C * M

RAW_COLS = PACK * H * W
assert RAW_COLS == O_TILES * C
SLOTS = 11

BK, BV, GAMMA, BETA, MEAN, VAR = 0, 1, 2, 3, 4, 5


def tile_nonlocalnd_bn_pa_t_kernel(
    tc, x, wk, bk, wv, bv, k_gamma, k_beta, k_mean, k_var, out_0, out_1
):
    nc = tc.nc
    with ExitStack() as ctx:
        const = ctx.enter_context(tc.tile_pool(name="const", bufs=1))
        slots = ctx.enter_context(tc.tile_pool(name="slots", bufs=1))
        taken = []

        def next_slot():
            taken.append(None)
            return "slot%d" % ((len(taken) - 1) % SLOTS)

        work = ctx.enter_context(tc.tile_pool(name="work", bufs=2))
        keep = ctx.enter_context(tc.tile_pool(name="keep", bufs=1))
        psum = ctx.enter_context(tc.psum_pool(name="psum", bufs=8))

        def load(src):
            raw = slots.tile([P, RAW_COLS], BF16, tag=next_slot(), align_bytes=256)
            nc.sync.dma_start(out=raw[:], in_=src)
            return raw

        def load_image(b):
            tiles = x[b].rearrange("(g p j) h w -> g p (j h w)", p=P, j=PACK)
            return [load(tiles[g]) for g in range(PASSES)]

        def load_weight(w):
            return load(w.rearrange("(p t) c -> p (t c)", t=O_TILES))

        def pool_and_quantise(x_raw):
            xp_codes = work.tile([P, PASSES, M], U32, align_bytes=64)
            xp_scales = work.tile([P, PASSES, M], U8, align_bytes=64)
            for g in range(PASSES):
                rows = x_raw[g][:].rearrange("p (r d w) -> p r d w", d=2, w=W)
                row_max = work.tile([P, RAW_COLS // 2], BF16)
                nc.vector.tensor_max(
                    out=row_max[:].rearrange("p (r w) -> p r w", w=W),
                    in0=rows[:, :, 0, :],
                    in1=rows[:, :, 1, :],
                )
                pairs = row_max[:].rearrange("p (j m d) -> p m j d", j=PACK, d=2)
                grouped = work.tile([P, M, PACK], BF16, align_bytes=64)
                nc.vector.tensor_max(out=grouped[:], in0=pairs[:, :, :, 0], in1=pairs[:, :, :, 1])
                nc.vector.quantize_mx(
                    out=xp_codes[:, g, :].bitcast(FP8X4),
                    scales=xp_scales[:, g, :],
                    in_=grouped[:].rearrange("p m j -> p (m j)"),
                )
            return xp_codes, xp_scales

        def quantise_weight(w_raw, name):
            w_codes = keep.tile([P, PASSES, O], U32, name=name + "_codes", align_bytes=64)
            w_scales = keep.tile([P, PASSES, O], U8, name=name + "_scales", align_bytes=64)
            words = w_raw[:].bitcast(F32).rearrange(
                "i (t g q u) -> i t g u q", t=O_TILES, g=PASSES, u=2
            )
            w_grouped = slots.tile([P, PASSES, O_TILES, P, PACK], BF16, tag=next_slot(), align_bytes=256)
            grouped_words = w_grouped[:].bitcast(F32)
            for g in range(PASSES):
                for t in range(0, O_TILES, 2):
                    bank = psum.tile([P, 2, 2, P], F32, tag="bank")
                    for d in range(2):
                        for u in range(2):
                            nc.tensor.transpose(bank[:, d, u, :], words[:, t + d, g, u, :], ident[:])
                    nc.scalar.copy(
                        out=grouped_words[:, g, t : t + 2, :, :],
                        in_=bank[:].rearrange("q d u i -> q d i u"),
                    )
                nc.vector.quantize_mx(
                    out=w_codes[:, g, :].bitcast(FP8X4),
                    scales=w_scales[:, g, :],
                    in_=w_grouped[:, g, :, :, :].rearrange("q t i j -> q (t i j)"),
                )
            return w_codes, w_scales

        def convolve(b, xp, weight, scale, shift, out):
            xp_codes, xp_scales = xp
            w_codes, w_scales = weight
            result = slots.tile([P, O_TILES, M], F32, tag=next_slot(), align_bytes=256)
            for t in range(O_TILES):
                cols = slice(t * P, (t + 1) * P)
                acc = psum.tile([P, M], F32, tag="bank")
                for g in range(PASSES):
                    nc.tensor.matmul_mx(
                        out=acc[:],
                        lhsT=w_codes[:, g, cols].bitcast(FP8X4),
                        lhsT_scale=w_scales[:, g, cols],
                        rhs=xp_codes[:, g, :].bitcast(FP8X4),
                        rhs_scale=xp_scales[:, g, :],
                        start=(g == 0),
                        stop=(g == PASSES - 1),
                    )
                nc.scalar.activation(
                    out=result[:, t, :],
                    in_=acc[:],
                    func=ACT.Identity,
                    scale=scale if isinstance(scale, float) else scale[:, t : t + 1],
                    bias=shift[:, t : t + 1],
                )
            queue = nc.scalar if (out is out_1 and b >= 1) else nc.sync
            queue.dma_start(
                out=out[b].rearrange("(p t) h w -> p (t h w)", t=O_TILES),
                in_=result[:].rearrange("p t m -> p (t m)"),
            )

        def fold_batch_norm():
            par = const.tile([P, 6, O_TILES], F32)
            nc.vector.tensor_copy(out=par[:], in_=par_raw[:, :, 0:6].rearrange("p t r -> p r t"))
            k_scale = const.tile([P, O_TILES], F32)
            k_shift = const.tile([P, O_TILES], F32)
            nc.vector.tensor_scalar_add(out=k_scale[:], in0=par[:, VAR, :], scalar1=EPS)
            nc.scalar.sqrt(k_scale[:], k_scale[:])
            nc.vector.reciprocal(out=k_scale[:], in_=k_scale[:])
            nc.vector.tensor_mul(out=k_scale[:], in0=k_scale[:], in1=par[:, GAMMA, :])
            nc.vector.tensor_sub(out=k_shift[:], in0=par[:, BK, :], in1=par[:, MEAN, :])
            nc.vector.tensor_mul(out=k_shift[:], in0=k_shift[:], in1=k_scale[:])
            nc.vector.tensor_add(out=k_shift[:], in0=k_shift[:], in1=par[:, BETA, :])
            return k_scale, k_shift, par[:, BV, :]

        x_raw = [load_image(0)]
        par_rows = const.tile([P, O], BF16)
        nc.vector.memset(par_rows[:], 0.0)
        for row, vec in ((BK, bk), (BV, bv), (GAMMA, k_gamma), (BETA, k_beta), (MEAN, k_mean), (VAR, k_var)):
            nc.sync.dma_start(out=par_rows[row : row + 1, :], in_=vec.rearrange("(a o) -> a o", a=1))
        wk_raw = load_weight(wk)
        wv_raw = load_weight(wv)
        x_raw.append(load_image(1))
        x_raw.append(load_image(2))

        ident = const.tile([P, P], F32)
        make_identity(nc, ident[:])
        ident_bf = const.tile([P, P], BF16)
        make_identity(nc, ident_bf[:])
        par_raw = psum.tile([P, O_TILES, P], BF16, tag="bank")
        par_cols = par_rows[:].rearrange("r (p t) -> r t p", t=O_TILES)
        for t in range(O_TILES):
            nc.tensor.transpose(par_raw[:, t, :], par_cols[:, t, :], ident_bf[:])

        xp = pool_and_quantise(x_raw[0])
        k_scale, k_shift, v_shift = fold_batch_norm()
        k_weight = quantise_weight(wk_raw, "wk")
        v_weight = quantise_weight(wv_raw, "wv")
        x_raw.append(load_image(3))
        for b in range(B):
            convolve(b, xp, k_weight, k_scale, k_shift, out_0)
            convolve(b, xp, v_weight, 1.0, v_shift, out_1)
            if b + 1 < B:
                xp = pool_and_quantise(x_raw[b + 1])
